import numpy as np
import ml_dtypes


def mxq(x, axis, fmt="e4m3"):
    dtype, down = {"e4m3": (ml_dtypes.float8_e4m3fn, 7), "e5m2": (ml_dtypes.float8_e5m2, 14)}[fmt]
    v = np.moveaxis(np.asarray(x, np.float32).astype(ml_dtypes.bfloat16).astype(np.float64), axis, -1)
    blocks = v.reshape(v.shape[:-1] + (-1, 32))
    amax = np.abs(blocks).max(-1, keepdims=True)
    byte = np.maximum(np.where(amax > 0, np.frexp(amax)[1] - 1 + 127, 0) - down, 1)
    scale = np.exp2(byte - 127.0)
    codes = (blocks / scale).astype(np.float32).astype(dtype).astype(np.float64)
    return np.moveaxis((codes * scale).reshape(v.shape), -1, axis)


WIDE = False


def mx_kscale(k, group=512):
    if not WIDE:
        return np.ones(k)
    levels = np.array([10, -10, 5, -5, 0])
    if group != 512:
        return np.exp2(np.random.permutation(np.resize(levels, k // group))).repeat(group)
    a = np.random.permutation(np.resize(levels, k // 512 * 4)).reshape(k // 512, 4)
    idx = np.arange(k)
    return np.exp2(a[idx // 512, idx % 128 // 32])


BF16 = ml_dtypes.bfloat16


def bf(x):
    return np.asarray(x, np.float32).astype(BF16)


def f64(x):
    return np.asarray(x).astype(np.float64)


B, S, E, H, KVH, D = 1, 512, 2048, 16, 4, 128
N_REP = H // KVH


def setup_inputs():
    u = mx_kscale(KVH * D, group=D).reshape(KVH, D)
    a = np.sqrt(2.0)
    sgn = np.where(np.random.standard_normal((KVH, D)) < 0.0, -1.0, 1.0)
    return {"q_rot": bf(np.random.standard_normal((B, S, H, D)) * a),
            "k_rot": bf(np.random.standard_normal((B, S, KVH, D)) * a),
            "v": bf((0.25 + 2.0 * np.random.random_sample((B, S, KVH, D))) * sgn * u),
            "wo_w": bf(np.random.standard_normal((E, H * D)) * np.sqrt(2.0 / (H * D)) / np.tile(u.reshape(-1), N_REP)[None, :])}


def reference(q_rot, k_rot, v, wo_w):
    q = f64(q_rot).reshape(B, S, N_REP, KVH, D).transpose(0, 2, 3, 1, 4)
    kt = f64(k_rot).transpose(0, 2, 3, 1)[:, None]
    vt = f64(v).transpose(0, 2, 1, 3)[:, None]
    s = (q @ kt) * (1.0 / np.sqrt(D))
    s = np.where(np.tril(np.ones((S, S), dtype=bool)), s, -np.inf)
    e = np.exp(s - s.max(-1, keepdims=True))
    o = (mxq(e, 4, "e4m3") @ mxq(vt, 3, "e4m3")) / e.sum(-1, keepdims=True)
    o = o.transpose(0, 3, 1, 2, 4).reshape(B, S, H * D)
    return mxq(o, 2, "e4m3") @ mxq(f64(wo_w), 1, "e4m3").T

@@ -1,0 +1,470 @@
+import math
+from contextlib import ExitStack
+
+import concourse.mybir as mybir
+from concourse.masks import make_identity
+
+F32 = mybir.dt.float32
+BF16 = mybir.dt.bfloat16
+I32 = mybir.dt.int32
+U32 = mybir.dt.uint32
+U8 = mybir.dt.uint8
+FP8X4 = mybir.dt.float8_e4m3fn_x4
+ALU = mybir.AluOpType
+ACT = mybir.ActivationFunctionType
+AXIS = mybir.AxisListType
+
+P = 128
+S = 512
+H = 16
+G = 4
+R = H // G
+D = 128
+E = 2048
+Q_TILES = S // P
+PASSES = (H * D) // (4 * P)
+N_OUT = 512
+OUT_BANKS = E // N_OUT
+ROW_TILES = N_OUT // P
+E_PADDED = 8
+SCORE_BANKS = 3
+SCALE = 1.0 / math.sqrt(D)
+MASKED = -1.0e30
+
+TILE_ORDER = (3, 0, 1, 2)
+
+LAG_MAX = 1
+LAG_EXP = 2
+LAG_TURN_E = 3
+LAG_QUANTISE_E = 4
+LAG_WEIGH = 5
+LAG_DIVIDE = 6
+LAG_TURN_O = 7
+LAG_QUANTISE_O = 8
+LAG_PROJECT = 9
+W_FIRST_TICK = 1
+W_UNITS_A_TICK = 2
+
+FLOPS = 2 * 2 * H * S * S * D + 2 * S * E * H * D
+
+
+def heads_in_pack(i):
+    return S // (P * (i + 1))
+
+
+def tile_attention_pb_kernel(tc, q_rot, k_rot, v, wo_w, out):
+    nc = tc.nc
+    with ExitStack() as ctx:
+        ctx.enter_context(tc.manual_schedule())
+        keep = ctx.enter_context(tc.tile_pool(name="keep", bufs=1))
+        stage = ctx.enter_context(tc.tile_pool(name="stage", bufs=2))
+        ps_scores = ctx.enter_context(tc.psum_pool(name="ps_scores", bufs=SCORE_BANKS))
+        ps_sums = ctx.enter_context(tc.psum_pool(name="ps_sums", bufs=1))
+        ps_bank = ctx.enter_context(tc.psum_pool(name="ps_bank", bufs=4))
+        live = {}
+
+        e_padded = keep.tile([P, E_PADDED, 2, S // 2], BF16)
+        nc.vector.memset(e_padded[:, :, :, 3 * S // 8 :], 0.0)
+        for i in range(Q_TILES - 1):
+            v_slots = keep.tile([P, 4, G * D], BF16, name="v_slots%d" % i)
+            nc.vector.memset(v_slots[:].rearrange("p t c -> p (t c)").bitcast(I32), 0)
+            live[("v_slots", i)] = v_slots
+        v_slots = keep.tile([P, 4, G * D], BF16, name="v_slots%d" % (Q_TILES - 1))
+        live[("v_slots", Q_TILES - 1)] = v_slots
+        warm_in = keep.tile([P, 1], F32)
+        warm_out = keep.tile([P, 1], F32)
+        nc.vector.memset(warm_in[:], 0.0)
+        nc.scalar.activation(out=warm_out[:], in_=warm_in[:], func=ACT.Exp)
+
+        ident_bf = keep.tile([P, P], BF16)
+        make_identity(nc, ident_bf[:])
+        ident_f32 = keep.tile([P, P], F32)
+        make_identity(nc, ident_f32[:])
+        mask_f32 = keep.tile([P, P], F32)
+        nc.gpsimd.memset(mask_f32[:], 0.0)
+        nc.gpsimd.affine_select(
+            out=mask_f32[:],
+            in_=mask_f32[:],
+            compare_op=ALU.is_ge,
+            fill=MASKED,
+            base=0,
+            pattern=[[-1, P]],
+            channel_multiplier=1,
+        )
+        mask_bf = keep.tile([P, P], BF16)
+        nc.vector.tensor_copy(out=mask_bf[:], in_=mask_f32[:])
+
+        row_max = keep.tile([P, Q_TILES * H], F32)
+        exp_bias = keep.tile([P, Q_TILES * H], F32)
+        row_sum = keep.tile([P, Q_TILES * H], F32)
+        row_inv = keep.tile([P, Q_TILES * H], F32)
+
+        def load_q(i):
+            q_rows = keep.tile([P, H * D], BF16, name="q_rows%d" % i)
+            nc.sync.dma_start(out=q_rows[:], in_=q_rot[0, i * P : (i + 1) * P].rearrange("s h d -> s (h d)"))
+            live[("q_rows", i)] = q_rows
+
+        def load_w_chunk(nn):
+            for t in range(ROW_TILES):
+                w_rows = stage.tile([P, H * D], BF16, tag="w_rows", bufs=2 * ROW_TILES)
+                first = nn * N_OUT + t * P
+                nc.sync.dma_start(out=w_rows[:], in_=wo_w[first : first + P, :])
+                live[("w_rows", nn, t)] = w_rows
+
+        def load_v(i):
+            n = P * (i + 1)
+            hp = heads_in_pack(i)
+            slots = live[("v_slots", i)]
+            for u in range(2):
+                keys = v[0, u * (n // 2) : (u + 1) * (n // 2)]
+                if hp == 1:
+                    nc.sync.dma_start(
+                        out=slots[0 : n // 4, 2 * u : 2 * u + 2, :],
+                        in_=keys.rearrange("(p e) g d -> p e (g d)", e=2),
+                    )
+                else:
+                    for g in range(G):
+                        first = (g % hp) * (P // hp)
+                        nc.sync.dma_start(
+                            out=slots[first : first + n // 4, 2 * u : 2 * u + 2, g * D : (g + 1) * D],
+                            in_=keys[:, g, :].rearrange("(p e) d -> p e d", e=2),
+                        )
+
+        k_rows = keep.tile([P, Q_TILES, G * D], BF16)
+        nc.sync.dma_start(out=k_rows[:], in_=k_rot[0].rearrange("(t p) g d -> p t (g d)", p=P))
+        load_q(TILE_ORDER[0])
+        load_w_chunk(0)
+        load_v(TILE_ORDER[0])
+        load_q(TILE_ORDER[1])
+        load_w_chunk(1)
+        for i in TILE_ORDER[2:]:
+            load_q(i)
+        for i in TILE_ORDER[1:]:
+            load_v(i)
+
+        kT = keep.tile([P, G, S], BF16)
+        for g in range(G):
+            turned = ps_bank.tile([P, Q_TILES, P], BF16, tag="bank")
+            for t in range(Q_TILES):
+                nc.tensor.transpose(turned[:, t, :], k_rows[:, t, g * D : (g + 1) * D], ident_bf[:])
+            nc.vector.tensor_copy(out=kT[:, g, :], in_=turned[:].rearrange("p t s -> p (t s)"))
+
+        def turn_q(i, r):
+            if r == 0:
+                qT = keep.tile([P, H, P], BF16, name="qT%d" % i)
+                live[("qT", i)] = qT
+            turned = ps_bank.tile([P, G, P], BF16, tag="bank")
+            for g in range(G):
+                h = G * r + g
+                nc.tensor.transpose(turned[:, g, :], live[("q_rows", i)][:, h * D : (h + 1) * D], ident_bf[:])
+            nc.scalar.copy(out=live[("qT", i)][:, G * r : G * (r + 1), :], in_=turned[:])
+
+        for r in range(R):
+            turn_q(TILE_ORDER[0], r)
+
+        def prepare_values(i):
+            v_grouped = stage.tile([P, G * D, 4], BF16, tag="v_grouped", align_bytes=64)
+            nc.vector.tensor_copy(out=v_grouped[:], in_=live[("v_slots", i)][:].rearrange("p t c -> p c t"))
+            v_codes = keep.tile([P, G * D], U32, name="v_codes%d" % i, align_bytes=64)
+            v_scales = keep.tile([P, G * D], U8, name="v_scales%d" % i, align_bytes=64)
+            nc.vector.quantize_mx(
+                out=v_codes[:].bitcast(FP8X4),
+                scales=v_scales[:],
+                in_=v_grouped[:].rearrange("p c t -> p (c t)"),
+            )
+            live[("v_codes", i)] = v_codes
+            live[("v_scales", i)] = v_scales
+
+        w_codes = keep.tile([P, PASSES, E], U32, align_bytes=64)
+        w_scales = keep.tile([P, PASSES, E], U8, align_bytes=64)
+
+        def turn_w(nn, half, t):
+            if t == 0:
+                w_grouped = stage.tile([P, 2, N_OUT, 4], BF16, tag="w_grouped", align_bytes=64)
+                live[("w_grouped", nn, half)] = w_grouped
+            words = live[("w_rows", nn, t)][:].bitcast(F32)
+            turned = ps_bank.tile([P, 2, 2, P], F32, tag="bank")
+            for cc in range(2):
+                c = 2 * half + cc
+                for u in range(2):
+                    nc.tensor.transpose(
+                        turned[:, cc, u, :], words[:, 256 * c + u : 256 * (c + 1) : 2], ident_f32[:]
+                    )
+            grouped_words = live[("w_grouped", nn, half)][:].rearrange("p c n t -> p (c n t)").bitcast(F32)
+            grouped_words = grouped_words.rearrange("p (c n u) -> p c n u", c=2, u=2)
+            copy = nc.vector.tensor_copy if t == ROW_TILES - 1 else nc.scalar.copy
+            copy(
+                out=grouped_words[:, :, t * P : (t + 1) * P, :],
+                in_=turned[:].rearrange("p c u n -> p c n u"),
+            )
+
+        def quantise_w(nn, half):
+            for cc in range(2):
+                c = 2 * half + cc
+                cols = slice(nn * N_OUT, (nn + 1) * N_OUT)
+                nc.vector.quantize_mx(
+                    out=w_codes[:, c, cols].bitcast(FP8X4),
+                    scales=w_scales[:, c, cols],
+                    in_=live[("w_grouped", nn, half)][:, cc].rearrange("p n t -> p (n t)"),
+                )
+
+        def score(i, r, pk):
+            n = P * (i + 1)
+            hp = heads_in_pack(i)
+            scores = ps_scores.tile([P, S], F32, tag="scores")
+            live[("scores", i, r, pk)] = scores
+            for j in range(hp):
+                g = pk * hp + j
+                queries = live[("qT", i)][:, G * r + g, :]
+                if i > 0:
+                    nc.tensor.matmul(
+                        scores[:, j * n : j * n + i * P],
+                        lhsT=queries,
+                        rhs=kT[:, g, 0 : i * P],
+                        start=True,
+                        stop=True,
+                    )
+                diagonal = scores[:, j * n + i * P : (j + 1) * n]
+                nc.tensor.matmul(diagonal, lhsT=queries, rhs=kT[:, g, i * P : n], start=True, stop=False)
+                nc.tensor.matmul(diagonal, lhsT=ident_bf[:], rhs=mask_bf[:], start=False, stop=True)
+
+        def find_max(i, r, pk):
+            n = P * (i + 1)
+            hp = heads_in_pack(i)
+            col = i * H + G * r + pk * hp
+            nc.vector.tensor_reduce(
+                out=row_max[:, col : col + hp],
+                in_=live[("scores", i, r, pk)][:, 0 : hp * n].rearrange("p (j n) -> p j n", j=hp),
+                axis=AXIS.X,
+                op=ALU.max,
+            )
+            nc.gpsimd.tensor_scalar(
+                out=exp_bias[:, col : col + hp],
+                in0=row_max[:, col : col + hp],
+                scalar1=-SCALE,
+                scalar2=0.0,
+                op0=ALU.mult,
+                op1=ALU.add,
+            )
+
+        def soften(i, r, pk):
+            n = P * (i + 1)
+            hp = heads_in_pack(i)
+            col = i * H + G * r + pk * hp
+            scores = live[("scores", i, r, pk)]
+            if n // 2 * hp < S // 2:
+                e_tile = e_padded[:, (G * r + pk) % E_PADDED].rearrange("p u k -> p (u k)")
+            else:
+                e_fresh = stage.tile([P, S], BF16, tag="e_tile", bufs=6)
+                e_tile = e_fresh[:]
+            live[("e", i, r, pk)] = e_tile
+            e_view = e_tile.rearrange("p (u j k) -> p u j k", u=2, j=hp)
+            for j in range(hp):
+                nc.scalar.activation(
+                    out=e_view[:, :, j, 0 : n // 2],
+                    in_=scores[:, j * n : (j + 1) * n].rearrange("p (u k) -> p u k", u=2),
+                    func=ACT.Exp,
+                    bias=exp_bias[:, col + j : col + j + 1],
+                    scale=SCALE,
+                    accum_out=row_sum[:, col + j : col + j + 1],
+                )
+
+        def turn_e(i, r, first, count):
+            if first == 0:
+                e_grouped = stage.tile([P, G * 4 * P], BF16, tag="e_grouped", align_bytes=64)
+                live[("e_grouped", i, r)] = e_grouped
+            e_words = live[("e_grouped", i, r)][:].bitcast(F32).rearrange("p (s q u) -> p s q u", s=G, u=2)
+            turned = ps_bank.tile([P, 2, 2, P], F32, tag="bank")
+            for s in range(count):
+                words = live[("e", i, r, first + s)].bitcast(F32)
+                for u in range(2):
+                    nc.tensor.transpose(turned[:, s, u, :], words[:, u * P : (u + 1) * P], ident_f32[:])
+            nc.scalar.copy(
+                out=e_words[:, first : first + count],
+                in_=turned[:, 0:count].rearrange("p s u q -> p s q u"),
+            )
+
+        def quantise_e(i, r):
+            packs_here = G // heads_in_pack(i)
+            e_codes = stage.tile([P, G * P], U32, tag="e_codes", align_bytes=64)
+            e_scales = stage.tile([P, G * P], U8, tag="e_scales", align_bytes=64)
+            nc.vector.quantize_mx(
+                out=e_codes[:, 0 : packs_here * P].bitcast(FP8X4),
+                scales=e_scales[:, 0 : packs_here * P],
+                in_=live[("e_grouped", i, r)][:, 0 : packs_here * 4 * P],
+            )
+            live[("e_codes", i, r)] = e_codes
+            live[("e_scales", i, r)] = e_scales
+
+        def weigh(i, r):
+            hp = heads_in_pack(i)
+            sums = ps_sums.tile([P, G * D], F32, tag="sums")
+            live[("sums", i, r)] = sums
+            for pk in range(G // hp):
+                rows = slice(pk * P, (pk + 1) * P)
+                cols = slice(pk * hp * D, (pk + 1) * hp * D)
+                nc.tensor.matmul_mx(
+                    out=sums[:, cols],
+                    lhsT=live[("e_codes", i, r)][:, rows].bitcast(FP8X4),
+                    lhsT_scale=live[("e_scales", i, r)][:, rows],
+                    rhs=live[("v_codes", i)][:, cols].bitcast(FP8X4),
+                    rhs_scale=live[("v_scales", i)][:, cols],
+                    start=True,
+                    stop=True,
+                )
+
+        def divide(i, r):
+            col = i * H + G * r
+            if r == 0:
+                o_sorted = stage.tile([P, PASSES, 2, 2 * P], BF16, tag="o_sorted")
+                live[("o_sorted", i)] = o_sorted
+            nc.vector.reciprocal(out=row_inv[:, col : col + G], in_=row_sum[:, col : col + G])
+            sums_view = live[("sums", i, r)][:].rearrange("q (g p u e) -> q u g p e", g=G, u=2, e=2)
+            inv_view = row_inv[:, col : col + G].unsqueeze(2).unsqueeze(3).to_broadcast([P, G, D // 4, 2])
+            for u in range(2):
+                nc.vector.tensor_tensor(
+                    out=live[("o_sorted", i)][:, r, u, :].rearrange("q (g p e) -> q g p e", g=G, e=2),
+                    in0=sums_view[:, u],
+                    in1=inv_view,
+                    op=ALU.mult,
+                )
+
+        def turn_o(i, r):
+            if r == 0:
+                o_grouped = stage.tile([P, PASSES * 4 * P], BF16, tag="o_grouped", align_bytes=64)
+                live[("o_grouped", i)] = o_grouped
+            turned = ps_bank.tile([P, 2, P], F32, tag="bank")
+            words = live[("o_sorted", i)][:, r].rearrange("q u k -> q (u k)").bitcast(F32)
+            for u in range(2):
+                nc.tensor.transpose(turned[:, u, :], words[:, u * P : (u + 1) * P], ident_f32[:])
+            o_words = live[("o_grouped", i)][:].bitcast(F32).rearrange("p (c q u) -> p c q u", c=PASSES, u=2)
+            nc.scalar.copy(out=o_words[:, r], in_=turned[:].rearrange("p u q -> p q u"))
+
+        def quantise_o(i, r):
+            if r == 0:
+                o_codes = stage.tile([P, PASSES * P], U32, tag="o_codes", align_bytes=64)
+                o_scales = stage.tile([P, PASSES * P], U8, tag="o_scales", align_bytes=64)
+                live[("o_codes", i)] = o_codes
+                live[("o_scales", i)] = o_scales
+            nc.vector.quantize_mx(
+                out=live[("o_codes", i)][:, r * P : (r + 1) * P].bitcast(FP8X4),
+                scales=live[("o_scales", i)][:, r * P : (r + 1) * P],
+                in_=live[("o_grouped", i)][:, r * 4 * P : (r + 1) * 4 * P],
+            )
+
+        def project_pass(i, nn, c):
+            rows = slice(c * P, (c + 1) * P)
+            cols = slice(nn * N_OUT, (nn + 1) * N_OUT)
+            nc.tensor.matmul_mx(
+                out=live[("acc", i, nn)][:],
+                lhsT=live[("o_codes", i)][:, rows].bitcast(FP8X4),
+                lhsT_scale=live[("o_scales", i)][:, rows],
+                rhs=w_codes[:, c, cols].bitcast(FP8X4),
+                rhs_scale=w_scales[:, c, cols],
+                start=(c == 0),
+                stop=(c == PASSES - 1),
+            )
+
+        def project_bank(i, nn):
+            acc = ps_bank.tile([P, N_OUT], F32, tag="bank")
+            live[("acc", i, nn)] = acc
+            for c in range(PASSES):
+                project_pass(i, nn, c)
+
+        def project_group(i, c):
+            for nn in range(OUT_BANKS):
+                if c == 0:
+                    if nn < SCORE_BANKS:
+                        acc = ps_scores.tile([P, N_OUT], F32, tag="scores")
+                    else:
+                        acc = ps_bank.tile([P, N_OUT], F32, tag="bank")
+                    live[("acc", i, nn)] = acc
+                project_pass(i, nn, c)
+
+        def store(i, nn):
+            result = stage.tile([P, N_OUT], F32, tag="result", bufs=4)
+            nc.scalar.copy(out=result[:], in_=live[("acc", i, nn)][:])
+            nc.sync.dma_start(out=out[0, i * P : (i + 1) * P, nn * N_OUT : (nn + 1) * N_OUT], in_=result[:])
+
+        packs = [(i, r, pk) for i in TILE_ORDER for r in range(R) for pk in range(G // heads_in_pack(i))]
+        w_units = [(nn, half, t) for nn in range(OUT_BANKS) for half in range(2) for t in range(ROW_TILES)]
+        last_tile = TILE_ORDER[-1]
+        scores_over = len(packs) + LAG_EXP
+
+        def pack_at(index):
+            return packs[index] if 0 <= index < len(packs) else None
+
+        def group_ending_at(index):
+            pack = pack_at(index)
+            if pack is not None and pack[2] == G // heads_in_pack(pack[0]) - 1:
+                return pack
+            return None
+
+        def w_units_of(tick):
+            first = (tick - W_FIRST_TICK) * W_UNITS_A_TICK
+            return w_units[first : first + W_UNITS_A_TICK] if first >= 0 else []
+
+        def banks_projected_in(tick):
+            found = []
+            for nn in range(OUT_BANKS):
+                pack = group_ending_at(tick - LAG_PROJECT - nn)
+                if pack is not None and pack[1] == R - 1 and pack[0] != last_tile:
+                    found.append((pack[0], nn))
+            if tick == len(packs) - 1 + LAG_PROJECT:
+                found.extend([(last_tile, nn) for nn in range(OUT_BANKS)])
+            return found
+
+        for tick in range(len(packs) + LAG_PROJECT + 1):
+            pack = pack_at(tick - LAG_MAX)
+            if pack is not None:
+                find_max(pack[0], pack[1], pack[2])
+            pack = pack_at(tick - LAG_EXP)
+            if pack is not None:
+                soften(pack[0], pack[1], pack[2])
+            for bank in banks_projected_in(tick - 1):
+                store(bank[0], bank[1])
+
+            pack = pack_at(tick - LAG_TURN_E)
+            if pack is not None and (pack[2] % 2 == 1 or group_ending_at(tick - LAG_TURN_E) is not None):
+                turn_e(pack[0], pack[1], pack[2] - pack[2] % 2, pack[2] % 2 + 1)
+            pack = group_ending_at(tick - LAG_TURN_O)
+            if pack is not None:
+                turn_o(pack[0], pack[1])
+            for unit in w_units_of(tick):
+                if unit[1] == 0 and unit[2] == 0 and 0 < unit[0] < OUT_BANKS - 1:
+                    load_w_chunk(unit[0] + 1)
+                turn_w(unit[0], unit[1], unit[2])
+            pack = group_ending_at(tick)
+            if pack is not None and pack[0] != last_tile:
+                turn_q(TILE_ORDER[TILE_ORDER.index(pack[0]) + 1], pack[1])
+            pack = pack_at(tick)
+            if pack is not None:
+                score(pack[0], pack[1], pack[2])
+
+            pack = group_ending_at(tick - LAG_QUANTISE_E)
+            if pack is not None:
+                quantise_e(pack[0], pack[1])
+            pack = group_ending_at(tick - LAG_DIVIDE)
+            if pack is not None:
+                divide(pack[0], pack[1])
+            pack = group_ending_at(tick - LAG_QUANTISE_O)
+            if pack is not None:
+                quantise_o(pack[0], pack[1])
+            for unit in w_units_of(tick - 1):
+                if unit[2] == ROW_TILES - 1:
+                    quantise_w(unit[0], unit[1])
+
+            pack = group_ending_at(tick - LAG_WEIGH)
+            if pack is not None:
+                weigh(pack[0], pack[1])
+            for bank in banks_projected_in(tick):
+                if bank[0] != last_tile:
+                    project_bank(bank[0], bank[1])
+            for index in range(len(packs)):
+                pack = group_ending_at(index)
+                if pack is not None and pack[0] == last_tile and tick == max(index + LAG_PROJECT, scores_over):
+                    project_group(last_tile, pack[1])
+
+            pack = pack_at(tick - 2)
+            if pack is not None and pack[1] == 0 and pack[2] == 0:
+                prepare_values(pack[0])

@@ -80,18 +80,18 @@ def tile_attention_pb_kernel(tc, q_rot, k_rot, v, wo_w, out):
         make_identity(nc, ident_bf[:])
         ident_f32 = keep.tile([P, P], F32)
         make_identity(nc, ident_f32[:])
-        mask_f32 = keep.tile([P, P], F32)
+        mask_f32 = keep.tile([P, S], F32)
         nc.gpsimd.memset(mask_f32[:], 0.0)
         nc.gpsimd.affine_select(
-            out=mask_f32[:],
-            in_=mask_f32[:],
+            out=mask_f32[:, S - P :],
+            in_=mask_f32[:, S - P :],
             compare_op=ALU.is_ge,
             fill=MASKED,
             base=0,
             pattern=[[-1, P]],
             channel_multiplier=1,
         )
-        mask_bf = keep.tile([P, P], BF16)
+        mask_bf = keep.tile([P, S], BF16)
         nc.vector.tensor_copy(out=mask_bf[:], in_=mask_f32[:])
 
         row_max = keep.tile([P, Q_TILES * H], F32)
@@ -216,17 +216,9 @@ def tile_attention_pb_kernel(tc, q_rot, k_rot, v, wo_w, out):
             for j in range(hp):
                 g = pk * hp + j
                 queries = live[("qT", i)][:, G * r + g, :]
-                if i > 0:
-                    nc.tensor.matmul(
-                        scores[:, j * n : j * n + i * P],
-                        lhsT=queries,
-                        rhs=kT[:, g, 0 : i * P],
-                        start=True,
-                        stop=True,
-                    )
-                diagonal = scores[:, j * n + i * P : (j + 1) * n]
-                nc.tensor.matmul(diagonal, lhsT=queries, rhs=kT[:, g, i * P : n], start=True, stop=False)
-                nc.tensor.matmul(diagonal, lhsT=ident_bf[:], rhs=mask_bf[:], start=False, stop=True)
+                row = scores[:, j * n : (j + 1) * n]
+                nc.tensor.matmul(row, lhsT=ident_bf[:], rhs=mask_bf[:, S - n :], start=True, stop=False)
+                nc.tensor.matmul(row, lhsT=queries, rhs=kT[:, g, 0:n], start=False, stop=True)
 
         def find_max(i, r, pk):
             n = P * (i + 1)

@@ -44,6 +44,7 @@ LAG_QUANTISE_O = 8
 LAG_PROJECT = 9
 W_FIRST_TICK = 1
 W_UNITS_A_TICK = 2
+PASSES_A_TICK = 2
 
 FLOPS = 2 * 2 * H * S * S * D + 2 * S * E * H * D
 
@@ -80,18 +81,18 @@ def tile_attention_pb_kernel(tc, q_rot, k_rot, v, wo_w, out):
         make_identity(nc, ident_bf[:])
         ident_f32 = keep.tile([P, P], F32)
         make_identity(nc, ident_f32[:])
-        mask_f32 = keep.tile([P, S], F32)
+        mask_f32 = keep.tile([P, P], F32)
         nc.gpsimd.memset(mask_f32[:], 0.0)
         nc.gpsimd.affine_select(
-            out=mask_f32[:, S - P :],
-            in_=mask_f32[:, S - P :],
+            out=mask_f32[:],
+            in_=mask_f32[:],
             compare_op=ALU.is_ge,
             fill=MASKED,
             base=0,
             pattern=[[-1, P]],
             channel_multiplier=1,
         )
-        mask_bf = keep.tile([P, S], BF16)
+        mask_bf = keep.tile([P, P], BF16)
         nc.vector.tensor_copy(out=mask_bf[:], in_=mask_f32[:])
 
         row_max = keep.tile([P, Q_TILES * H], F32)
@@ -137,10 +138,12 @@ def tile_attention_pb_kernel(tc, q_rot, k_rot, v, wo_w, out):
         load_v(TILE_ORDER[0])
         load_q(TILE_ORDER[1])
         load_w_chunk(1)
-        for i in TILE_ORDER[2:]:
-            load_q(i)
-        for i in TILE_ORDER[1:]:
-            load_v(i)
+
+        def load_the_rest():
+            load_v(TILE_ORDER[1])
+            for i in TILE_ORDER[2:]:
+                load_q(i)
+                load_v(i)
 
         kT = keep.tile([P, G, S], BF16)
         for g in range(G):
@@ -159,8 +162,7 @@ def tile_attention_pb_kernel(tc, q_rot, k_rot, v, wo_w, out):
                 nc.tensor.transpose(turned[:, g, :], live[("q_rows", i)][:, h * D : (h + 1) * D], ident_bf[:])
             nc.scalar.copy(out=live[("qT", i)][:, G * r : G * (r + 1), :], in_=turned[:])
 
-        for r in range(R):
-            turn_q(TILE_ORDER[0], r)
+        turn_q(TILE_ORDER[0], 0)
 
         def prepare_values(i):
             v_grouped = stage.tile([P, G * D, 4], BF16, tag="v_grouped", align_bytes=64)
@@ -216,9 +218,17 @@ def tile_attention_pb_kernel(tc, q_rot, k_rot, v, wo_w, out):
             for j in range(hp):
                 g = pk * hp + j
                 queries = live[("qT", i)][:, G * r + g, :]
-                row = scores[:, j * n : (j + 1) * n]
-                nc.tensor.matmul(row, lhsT=ident_bf[:], rhs=mask_bf[:, S - n :], start=True, stop=False)
-                nc.tensor.matmul(row, lhsT=queries, rhs=kT[:, g, 0:n], start=False, stop=True)
+                if i > 0:
+                    nc.tensor.matmul(
+                        scores[:, j * n : j * n + i * P],
+                        lhsT=queries,
+                        rhs=kT[:, g, 0 : i * P],
+                        start=True,
+                        stop=True,
+                    )
+                diagonal = scores[:, j * n + i * P : (j + 1) * n]
+                nc.tensor.matmul(diagonal, lhsT=queries, rhs=kT[:, g, i * P : n], start=True, stop=False)
+                nc.tensor.matmul(diagonal, lhsT=ident_bf[:], rhs=mask_bf[:], start=False, stop=True)
 
         def find_max(i, r, pk):
             n = P * (i + 1)
@@ -230,13 +240,8 @@ def tile_attention_pb_kernel(tc, q_rot, k_rot, v, wo_w, out):
                 axis=AXIS.X,
                 op=ALU.max,
             )
-            nc.gpsimd.tensor_scalar(
-                out=exp_bias[:, col : col + hp],
-                in0=row_max[:, col : col + hp],
-                scalar1=-SCALE,
-                scalar2=0.0,
-                op0=ALU.mult,
-                op1=ALU.add,
+            nc.vector.tensor_scalar_mul(
+                out=exp_bias[:, col : col + hp], in0=row_max[:, col : col + hp], scalar1=-SCALE
             )
 
         def soften(i, r, pk):
@@ -278,6 +283,8 @@ def tile_attention_pb_kernel(tc, q_rot, k_rot, v, wo_w, out):
 
         def quantise_e(i, r):
             packs_here = G // heads_in_pack(i)
+            col = i * H + G * r
+            nc.vector.reciprocal(out=row_inv[:, col : col + G], in_=row_sum[:, col : col + G])
             e_codes = stage.tile([P, G * P], U32, tag="e_codes", align_bytes=64)
             e_scales = stage.tile([P, G * P], U8, tag="e_scales", align_bytes=64)
             nc.vector.quantize_mx(
@@ -310,7 +317,6 @@ def tile_attention_pb_kernel(tc, q_rot, k_rot, v, wo_w, out):
             if r == 0:
                 o_sorted = stage.tile([P, PASSES, 2, 2 * P], BF16, tag="o_sorted")
                 live[("o_sorted", i)] = o_sorted
-            nc.vector.reciprocal(out=row_inv[:, col : col + G], in_=row_sum[:, col : col + G])
             sums_view = live[("sums", i, r)][:].rearrange("q (g p u e) -> q u g p e", g=G, u=2, e=2)
             inv_view = row_inv[:, col : col + G].unsqueeze(2).unsqueeze(3).to_broadcast([P, G, D // 4, 2])
             for u in range(2):
@@ -334,8 +340,8 @@ def tile_attention_pb_kernel(tc, q_rot, k_rot, v, wo_w, out):
 
         def quantise_o(i, r):
             if r == 0:
-                o_codes = stage.tile([P, PASSES * P], U32, tag="o_codes", align_bytes=64)
-                o_scales = stage.tile([P, PASSES * P], U8, tag="o_scales", align_bytes=64)
+                o_codes = stage.tile([P, PASSES * P], U32, tag="o_codes", align_bytes=64, bufs=3)
+                o_scales = stage.tile([P, PASSES * P], U8, tag="o_scales", align_bytes=64, bufs=3)
                 live[("o_codes", i)] = o_codes
                 live[("o_scales", i)] = o_scales
             nc.vector.quantize_mx(
@@ -345,6 +351,12 @@ def tile_attention_pb_kernel(tc, q_rot, k_rot, v, wo_w, out):
             )
 
         def project_pass(i, nn, c):
+            if c == 0:
+                if i == TILE_ORDER[-1] and nn < SCORE_BANKS:
+                    acc = ps_scores.tile([P, N_OUT], F32, tag="scores")
+                else:
+                    acc = ps_bank.tile([P, N_OUT], F32, tag="bank")
+                live[("acc", i, nn)] = acc
             rows = slice(c * P, (c + 1) * P)
             cols = slice(nn * N_OUT, (nn + 1) * N_OUT)
             nc.tensor.matmul_mx(
@@ -357,25 +369,10 @@ def tile_attention_pb_kernel(tc, q_rot, k_rot, v, wo_w, out):
                 stop=(c == PASSES - 1),
             )
 
-        def project_bank(i, nn):
-            acc = ps_bank.tile([P, N_OUT], F32, tag="bank")
-            live[("acc", i, nn)] = acc
-            for c in range(PASSES):
-                project_pass(i, nn, c)
-
-        def project_group(i, c):
-            for nn in range(OUT_BANKS):
-                if c == 0:
-                    if nn < SCORE_BANKS:
-                        acc = ps_scores.tile([P, N_OUT], F32, tag="scores")
-                    else:
-                        acc = ps_bank.tile([P, N_OUT], F32, tag="bank")
-                    live[("acc", i, nn)] = acc
-                project_pass(i, nn, c)
-
         def store(i, nn):
             result = stage.tile([P, N_OUT], F32, tag="result", bufs=4)
-            nc.scalar.copy(out=result[:], in_=live[("acc", i, nn)][:])
+            copy = nc.vector.tensor_copy if i == TILE_ORDER[-1] and nn % 2 == 1 else nc.scalar.copy
+            copy(out=result[:], in_=live[("acc", i, nn)][:])
             nc.sync.dma_start(out=out[0, i * P : (i + 1) * P, nn * N_OUT : (nn + 1) * N_OUT], in_=result[:])
 
         packs = [(i, r, pk) for i in TILE_ORDER for r in range(R) for pk in range(G // heads_in_pack(i))]
@@ -396,14 +393,19 @@ def tile_attention_pb_kernel(tc, q_rot, k_rot, v, wo_w, out):
             first = (tick - W_FIRST_TICK) * W_UNITS_A_TICK
             return w_units[first : first + W_UNITS_A_TICK] if first >= 0 else []
 
-        def banks_projected_in(tick):
+        first_project_tick = R * (G // heads_in_pack(TILE_ORDER[0])) - 1 + LAG_PROJECT
+
+        def passes_of(tick):
             found = []
-            for nn in range(OUT_BANKS):
-                pack = group_ending_at(tick - LAG_PROJECT - nn)
-                if pack is not None and pack[1] == R - 1 and pack[0] != last_tile:
-                    found.append((pack[0], nn))
-            if tick == len(packs) - 1 + LAG_PROJECT:
-                found.extend([(last_tile, nn) for nn in range(OUT_BANKS)])
+            per_tile = OUT_BANKS * PASSES
+            first = (tick - first_project_tick) * PASSES_A_TICK
+            for number in range(max(first, 0), min(first + PASSES_A_TICK, (Q_TILES - 1) * per_tile)):
+                found.append((TILE_ORDER[number // per_tile], number % per_tile // PASSES, number % PASSES))
+            for index in range(len(packs)):
+                pack = group_ending_at(index)
+                if pack is not None and pack[0] == last_tile:
+                    if tick == max(index + LAG_PROJECT, scores_over + 2 * pack[1]):
+                        found.extend([(last_tile, nn, pack[1]) for nn in range(OUT_BANKS)])
             return found
 
         for tick in range(len(packs) + LAG_PROJECT + 1):
@@ -413,8 +415,9 @@ def tile_attention_pb_kernel(tc, q_rot, k_rot, v, wo_w, out):
             pack = pack_at(tick - LAG_EXP)
             if pack is not None:
                 soften(pack[0], pack[1], pack[2])
-            for bank in banks_projected_in(tick - 1):
-                store(bank[0], bank[1])
+            for done in passes_of(tick - 1):
+                if done[2] == PASSES - 1:
+                    store(done[0], done[1])
 
             pack = pack_at(tick - LAG_TURN_E)
             if pack is not None and (pack[2] % 2 == 1 or group_ending_at(tick - LAG_TURN_E) is not None):
@@ -425,7 +428,11 @@ def tile_attention_pb_kernel(tc, q_rot, k_rot, v, wo_w, out):
             for unit in w_units_of(tick):
                 if unit[1] == 0 and unit[2] == 0 and 0 < unit[0] < OUT_BANKS - 1:
                     load_w_chunk(unit[0] + 1)
+                    if unit[0] + 1 == OUT_BANKS - 1:
+                        load_the_rest()
                 turn_w(unit[0], unit[1], unit[2])
+            if tick + 1 < R:
+                turn_q(TILE_ORDER[0], tick + 1)
             pack = group_ending_at(tick)
             if pack is not None and pack[0] != last_tile:
                 turn_q(TILE_ORDER[TILE_ORDER.index(pack[0]) + 1], pack[1])
@@ -449,13 +456,8 @@ def tile_attention_pb_kernel(tc, q_rot, k_rot, v, wo_w, out):
             pack = group_ending_at(tick - LAG_WEIGH)
             if pack is not None:
                 weigh(pack[0], pack[1])
-            for bank in banks_projected_in(tick):
-                if bank[0] != last_tile:
-                    project_bank(bank[0], bank[1])
-            for index in range(len(packs)):
-                pack = group_ending_at(index)
-                if pack is not None and pack[0] == last_tile and tick == max(index + LAG_PROJECT, scores_over):
-                    project_group(last_tile, pack[1])
+            for due in passes_of(tick):
+                project_pass(due[0], due[1], due[2])
 
             pack = pack_at(tick - 2)
             if pack is not None and pack[1] == 0 and pack[2] == 0:

@@ -56,7 +56,6 @@ def heads_in_pack(i):
 def tile_attention_pb_kernel(tc, q_rot, k_rot, v, wo_w, out):
     nc = tc.nc
     with ExitStack() as ctx:
-        ctx.enter_context(tc.manual_schedule())
         keep = ctx.enter_context(tc.tile_pool(name="keep", bufs=1))
         stage = ctx.enter_context(tc.tile_pool(name="stage", bufs=2))
         ps_scores = ctx.enter_context(tc.psum_pool(name="ps_scores", bufs=SCORE_BANKS))

@@ -12,7 +12,6 @@ U8 = mybir.dt.uint8
 FP8X4 = mybir.dt.float8_e4m3fn_x4
 ALU = mybir.AluOpType
 ACT = mybir.ActivationFunctionType
-AXIS = mybir.AxisListType
 
 P = 128
 S = 512
@@ -94,7 +93,6 @@ def tile_attention_pb_kernel(tc, q_rot, k_rot, v, wo_w, out):
         mask_bf = keep.tile([P, P], BF16)
         nc.vector.tensor_copy(out=mask_bf[:], in_=mask_f32[:])
 
-        row_max = keep.tile([P, Q_TILES * H], F32)
         exp_bias = keep.tile([P, Q_TILES * H], F32)
         row_sum = keep.tile([P, Q_TILES * H], F32)
         row_inv = keep.tile([P, Q_TILES * H], F32)
@@ -233,15 +231,17 @@ def tile_attention_pb_kernel(tc, q_rot, k_rot, v, wo_w, out):
             n = P * (i + 1)
             hp = heads_in_pack(i)
             col = i * H + G * r + pk * hp
-            nc.vector.tensor_reduce(
-                out=row_max[:, col : col + hp],
-                in_=live[("scores", i, r, pk)][:, 0 : hp * n].rearrange("p (j n) -> p j n", j=hp),
-                axis=AXIS.X,
-                op=ALU.max,
-            )
-            nc.vector.tensor_scalar_mul(
-                out=exp_bias[:, col : col + hp], in0=row_max[:, col : col + hp], scalar1=-SCALE
-            )
+            for j in range(hp):
+                unused = stage.tile([P, S], BF16, tag="unused", bufs=4)
+                nc.vector.tensor_scalar(
+                    out=unused[:, 0:n],
+                    in0=live[("scores", i, r, pk)][:, j * n : (j + 1) * n],
+                    scalar1=-SCALE,
+                    scalar2=None,
+                    op0=ALU.mult,
+                    op1=ALU.min,
+                    accum_out=exp_bias[:, col + j : col + j + 1],
+                )
 
         def soften(i, r, pk):
             n = P * (i + 1)
@@ -392,14 +392,23 @@ def tile_attention_pb_kernel(tc, q_rot, k_rot, v, wo_w, out):
             first = (tick - W_FIRST_TICK) * W_UNITS_A_TICK
             return w_units[first : first + W_UNITS_A_TICK] if first >= 0 else []
 
-        first_project_tick = R * (G // heads_in_pack(TILE_ORDER[0])) - 1 + LAG_PROJECT
+        per_tile = OUT_BANKS * PASSES
+        project_from = []
+        for index in range(len(packs)):
+            pack = group_ending_at(index)
+            if pack is not None and pack[1] == R - 1 and pack[0] != last_tile:
+                ready = index + LAG_PROJECT
+                if project_from:
+                    ready = max(ready, project_from[-1] + per_tile // PASSES_A_TICK)
+                project_from.append(ready)
+        last_tick = max(len(packs) - 1 + LAG_PROJECT, scores_over + 2 * (R - 1), project_from[-1] + per_tile // PASSES_A_TICK)
 
         def passes_of(tick):
             found = []
-            per_tile = OUT_BANKS * PASSES
-            first = (tick - first_project_tick) * PASSES_A_TICK
-            for number in range(max(first, 0), min(first + PASSES_A_TICK, (Q_TILES - 1) * per_tile)):
-                found.append((TILE_ORDER[number // per_tile], number % per_tile // PASSES, number % PASSES))
+            for k in range(Q_TILES - 1):
+                first = (tick - project_from[k]) * PASSES_A_TICK
+                for number in range(max(first, 0), min(first + PASSES_A_TICK, per_tile)):
+                    found.append((TILE_ORDER[k], number // PASSES, number % PASSES))
             for index in range(len(packs)):
                 pack = group_ending_at(index)
                 if pack is not None and pack[0] == last_tile:
@@ -407,7 +416,7 @@ def tile_attention_pb_kernel(tc, q_rot, k_rot, v, wo_w, out):
                         found.extend([(last_tile, nn, pack[1]) for nn in range(OUT_BANKS)])
             return found
 
-        for tick in range(len(packs) + LAG_PROJECT + 1):
+        for tick in range(last_tick + 2):
             pack = pack_at(tick - LAG_MAX)
             if pack is not None:
                 find_max(pack[0], pack[1], pack[2])

@@ -97,9 +97,16 @@ def tile_attention_pb_kernel(tc, q_rot, k_rot, v, wo_w, out):
         row_sum = keep.tile([P, Q_TILES * H], F32)
         row_inv = keep.tile([P, Q_TILES * H], F32)
 
-        def load_q(i):
+        def load_q(i, pieces):
             q_rows = keep.tile([P, H * D], BF16, name="q_rows%d" % i)
-            nc.sync.dma_start(out=q_rows[:], in_=q_rot[0, i * P : (i + 1) * P].rearrange("s h d -> s (h d)"))
+            heads = H // pieces
+            for piece in range(pieces):
+                nc.sync.dma_start(
+                    out=q_rows[:, piece * heads * D : (piece + 1) * heads * D],
+                    in_=q_rot[0, i * P : (i + 1) * P, piece * heads : (piece + 1) * heads, :].rearrange(
+                        "s h d -> s (h d)"
+                    ),
+                )
             live[("q_rows", i)] = q_rows
 
         def load_w_chunk(nn):
@@ -130,16 +137,16 @@ def tile_attention_pb_kernel(tc, q_rot, k_rot, v, wo_w, out):
 
         k_rows = keep.tile([P, Q_TILES, G * D], BF16)
         nc.sync.dma_start(out=k_rows[:], in_=k_rot[0].rearrange("(t p) g d -> p t (g d)", p=P))
-        load_q(TILE_ORDER[0])
+        load_q(TILE_ORDER[0], R)
         load_w_chunk(0)
         load_v(TILE_ORDER[0])
-        load_q(TILE_ORDER[1])
+        load_q(TILE_ORDER[1], 1)
         load_w_chunk(1)
 
         def load_the_rest():
             load_v(TILE_ORDER[1])
             for i in TILE_ORDER[2:]:
-                load_q(i)
+                load_q(i, 1)
                 load_v(i)
 
         kT = keep.tile([P, G, S], BF16)
@@ -161,15 +168,18 @@ def tile_attention_pb_kernel(tc, q_rot, k_rot, v, wo_w, out):
 
         turn_q(TILE_ORDER[0], 0)
 
-        def prepare_values(i):
+        def group_values(i):
             v_grouped = stage.tile([P, G * D, 4], BF16, tag="v_grouped", align_bytes=64)
             nc.vector.tensor_copy(out=v_grouped[:], in_=live[("v_slots", i)][:].rearrange("p t c -> p c t"))
+            live[("v_grouped", i)] = v_grouped
+
+        def quantise_values(i):
             v_codes = keep.tile([P, G * D], U32, name="v_codes%d" % i, align_bytes=64)
             v_scales = keep.tile([P, G * D], U8, name="v_scales%d" % i, align_bytes=64)
             nc.vector.quantize_mx(
                 out=v_codes[:].bitcast(FP8X4),
                 scales=v_scales[:],
-                in_=v_grouped[:].rearrange("p c t -> p (c t)"),
+                in_=live[("v_grouped", i)][:].rearrange("p c t -> p (c t)"),
             )
             live[("v_codes", i)] = v_codes
             live[("v_scales", i)] = v_scales
@@ -231,10 +241,11 @@ def tile_attention_pb_kernel(tc, q_rot, k_rot, v, wo_w, out):
             n = P * (i + 1)
             hp = heads_in_pack(i)
             col = i * H + G * r + pk * hp
+            scaled = stage.tile([P, S], F32, tag="scaled", bufs=4)
+            live[("scaled", i, r, pk)] = scaled
             for j in range(hp):
-                unused = stage.tile([P, S], BF16, tag="unused", bufs=4)
                 nc.vector.tensor_scalar(
-                    out=unused[:, 0:n],
+                    out=scaled[:, j * n : (j + 1) * n],
                     in0=live[("scores", i, r, pk)][:, j * n : (j + 1) * n],
                     scalar1=-SCALE,
                     scalar2=None,
@@ -247,7 +258,7 @@ def tile_attention_pb_kernel(tc, q_rot, k_rot, v, wo_w, out):
             n = P * (i + 1)
             hp = heads_in_pack(i)
             col = i * H + G * r + pk * hp
-            scores = live[("scores", i, r, pk)]
+            scaled = live[("scaled", i, r, pk)]
             if n // 2 * hp < S // 2:
                 e_tile = e_padded[:, (G * r + pk) % E_PADDED].rearrange("p u k -> p (u k)")
             else:
@@ -258,10 +269,10 @@ def tile_attention_pb_kernel(tc, q_rot, k_rot, v, wo_w, out):
             for j in range(hp):
                 nc.scalar.activation(
                     out=e_view[:, :, j, 0 : n // 2],
-                    in_=scores[:, j * n : (j + 1) * n].rearrange("p (u k) -> p u k", u=2),
+                    in_=scaled[:, j * n : (j + 1) * n].rearrange("p (u k) -> p u k", u=2),
                     func=ACT.Exp,
                     bias=exp_bias[:, col + j : col + j + 1],
-                    scale=SCALE,
+                    scale=-1.0,
                     accum_out=row_sum[:, col + j : col + j + 1],
                 )
 
@@ -377,7 +388,7 @@ def tile_attention_pb_kernel(tc, q_rot, k_rot, v, wo_w, out):
         packs = [(i, r, pk) for i in TILE_ORDER for r in range(R) for pk in range(G // heads_in_pack(i))]
         w_units = [(nn, half, t) for nn in range(OUT_BANKS) for half in range(2) for t in range(ROW_TILES)]
         last_tile = TILE_ORDER[-1]
-        scores_over = len(packs) + LAG_EXP
+        scores_over = len(packs) + LAG_MAX
 
         def pack_at(index):
             return packs[index] if 0 <= index < len(packs) else None
@@ -469,4 +480,7 @@ def tile_attention_pb_kernel(tc, q_rot, k_rot, v, wo_w, out):
 
             pack = pack_at(tick - 2)
             if pack is not None and pack[1] == 0 and pack[2] == 0:
-                prepare_values(pack[0])
+                quantise_values(pack[0])
+            pack = pack_at(tick - 1)
+            if pack is not None and pack[1] == 0 and pack[2] == 0:
+                group_values(pack[0])

@@ -26,6 +26,7 @@ N_OUT = 512
 OUT_BANKS = E // N_OUT
 ROW_TILES = N_OUT // P
 E_PADDED = 8
+V_LAYOUT = (0, 1, 3, 3)
 SCORE_BANKS = 3
 SCALE = 1.0 / math.sqrt(D)
 MASKED = -1.0e30
@@ -40,9 +41,11 @@ LAG_WEIGH = 5
 LAG_DIVIDE = 6
 LAG_TURN_O = 7
 LAG_QUANTISE_O = 8
+LAG_TURN_Q = 2
+LAG_VALUES = 2
 LAG_PROJECT = 9
 W_FIRST_TICK = 1
-W_UNITS_A_TICK = 2
+W_UNITS_A_TICK = 1.25
 PASSES_A_TICK = 2
 
 FLOPS = 2 * 2 * H * S * S * D + 2 * S * E * H * D
@@ -62,9 +65,9 @@ def tile_attention_pb_kernel(tc, q_rot, k_rot, v, wo_w, out):
         ps_bank = ctx.enter_context(tc.psum_pool(name="ps_bank", bufs=4))
         live = {}
 
-        e_padded = keep.tile([P, E_PADDED, 2, S // 2], BF16)
-        nc.vector.memset(e_padded[:, :, :, 3 * S // 8 :], 0.0)
-        for i in range(Q_TILES - 1):
+        e_padded = keep.tile([P, E_PADDED, S], BF16)
+        nc.vector.memset(e_padded[:, :, 3 * S // 4 :], 0.0)
+        for i in range(2):
             v_slots = keep.tile([P, 4, G * D], BF16, name="v_slots%d" % i)
             nc.vector.memset(v_slots[:].rearrange("p t c -> p (t c)").bitcast(I32), 0)
             live[("v_slots", i)] = v_slots
@@ -97,17 +100,14 @@ def tile_attention_pb_kernel(tc, q_rot, k_rot, v, wo_w, out):
         row_sum = keep.tile([P, Q_TILES * H], F32)
         row_inv = keep.tile([P, Q_TILES * H], F32)
 
-        def load_q(i, pieces):
-            q_rows = keep.tile([P, H * D], BF16, name="q_rows%d" % i)
-            heads = H // pieces
-            for piece in range(pieces):
-                nc.sync.dma_start(
-                    out=q_rows[:, piece * heads * D : (piece + 1) * heads * D],
-                    in_=q_rot[0, i * P : (i + 1) * P, piece * heads : (piece + 1) * heads, :].rearrange(
-                        "s h d -> s (h d)"
-                    ),
-                )
-            live[("q_rows", i)] = q_rows
+        def load_q(i, first, count):
+            if first == 0:
+                q_rows = keep.tile([P, H * D], BF16, name="q_rows%d" % i)
+                live[("q_rows", i)] = q_rows
+            nc.sync.dma_start(
+                out=live[("q_rows", i)][:, first * D : (first + count) * D],
+                in_=q_rot[0, i * P : (i + 1) * P, first : first + count, :].rearrange("s h d -> s (h d)"),
+            )
 
         def load_w_chunk(nn):
             for t in range(ROW_TILES):
@@ -135,26 +135,21 @@ def tile_attention_pb_kernel(tc, q_rot, k_rot, v, wo_w, out):
                             in_=keys[:, g, :].rearrange("(p e) d -> p e d", e=2),
                         )
 
+        load_q(TILE_ORDER[0], 0, G)
         k_rows = keep.tile([P, Q_TILES, G * D], BF16)
-        nc.sync.dma_start(out=k_rows[:], in_=k_rot[0].rearrange("(t p) g d -> p t (g d)", p=P))
-        load_q(TILE_ORDER[0], R)
+        for t in range(Q_TILES):
+            nc.sync.dma_start(out=k_rows[:, t, :], in_=k_rot[0, t * P : (t + 1) * P].rearrange("p g d -> p (g d)"))
+        for r in range(1, R):
+            load_q(TILE_ORDER[0], G * r, G)
         load_w_chunk(0)
         load_v(TILE_ORDER[0])
-        load_q(TILE_ORDER[1], 1)
+        load_q(TILE_ORDER[1], 0, H)
         load_w_chunk(1)
-
-        def load_the_rest():
-            load_v(TILE_ORDER[1])
-            for i in TILE_ORDER[2:]:
-                load_q(i, 1)
+        load_v(TILE_ORDER[1])
+        for i in TILE_ORDER[2:]:
+            load_q(i, 0, H)
+            if V_LAYOUT[i] == i:
                 load_v(i)
-
-        kT = keep.tile([P, G, S], BF16)
-        for g in range(G):
-            turned = ps_bank.tile([P, Q_TILES, P], BF16, tag="bank")
-            for t in range(Q_TILES):
-                nc.tensor.transpose(turned[:, t, :], k_rows[:, t, g * D : (g + 1) * D], ident_bf[:])
-            nc.vector.tensor_copy(out=kT[:, g, :], in_=turned[:].rearrange("p t s -> p (t s)"))
 
         def turn_q(i, r):
             if r == 0:
@@ -168,9 +163,28 @@ def tile_attention_pb_kernel(tc, q_rot, k_rot, v, wo_w, out):
 
         turn_q(TILE_ORDER[0], 0)
 
+        kT = keep.tile([P, G, S], BF16)
+        k_turned = []
+        for g in range(G):
+            bank = ps_bank.tile([P, Q_TILES, P], BF16, tag="bank")
+            k_turned.append(bank)
+        for t in range(Q_TILES):
+            for g in range(G):
+                nc.tensor.transpose(k_turned[g][:, t, :], k_rows[:, t, g * D : (g + 1) * D], ident_bf[:])
+        for g in range(G):
+            copy = nc.vector.tensor_copy if g % 2 == 0 else nc.scalar.copy
+            copy(out=kT[:, g, :], in_=k_turned[g][:].rearrange("p t s -> p (t s)"))
+
         def group_values(i):
             v_grouped = stage.tile([P, G * D, 4], BF16, tag="v_grouped", align_bytes=64)
-            nc.vector.tensor_copy(out=v_grouped[:], in_=live[("v_slots", i)][:].rearrange("p t c -> p c t"))
+            nc.gpsimd.tensor_scalar(
+                out=v_grouped[:],
+                in0=live[("v_slots", i)][:].rearrange("p t c -> p c t"),
+                scalar1=1.0,
+                scalar2=0.0,
+                op0=ALU.mult,
+                op1=ALU.add,
+            )
             live[("v_grouped", i)] = v_grouped
 
         def quantise_values(i):
@@ -259,17 +273,18 @@ def tile_attention_pb_kernel(tc, q_rot, k_rot, v, wo_w, out):
             hp = heads_in_pack(i)
             col = i * H + G * r + pk * hp
             scaled = live[("scaled", i, r, pk)]
-            if n // 2 * hp < S // 2:
-                e_tile = e_padded[:, (G * r + pk) % E_PADDED].rearrange("p u k -> p (u k)")
+            if n * hp < S:
+                e_tile = e_padded[:, (G * r + pk) % E_PADDED]
             else:
                 e_fresh = stage.tile([P, S], BF16, tag="e_tile", bufs=6)
                 e_tile = e_fresh[:]
             live[("e", i, r, pk)] = e_tile
             e_view = e_tile.rearrange("p (u j k) -> p u j k", u=2, j=hp)
             for j in range(hp):
+                exponents = scaled[:, j * n : (j + 1) * n]
                 nc.scalar.activation(
-                    out=e_view[:, :, j, 0 : n // 2],
-                    in_=scaled[:, j * n : (j + 1) * n].rearrange("p (u k) -> p u k", u=2),
+                    out=e_tile[:, 0:n] if hp == 1 else e_view[:, :, j],
+                    in_=exponents if hp == 1 else exponents.rearrange("p (u k) -> p u k", u=2),
                     func=ACT.Exp,
                     bias=exp_bias[:, col + j : col + j + 1],
                     scale=-1.0,
@@ -316,8 +331,8 @@ def tile_attention_pb_kernel(tc, q_rot, k_rot, v, wo_w, out):
                     out=sums[:, cols],
                     lhsT=live[("e_codes", i, r)][:, rows].bitcast(FP8X4),
                     lhsT_scale=live[("e_scales", i, r)][:, rows],
-                    rhs=live[("v_codes", i)][:, cols].bitcast(FP8X4),
-                    rhs_scale=live[("v_scales", i)][:, cols],
+                    rhs=live[("v_codes", V_LAYOUT[i])][:, cols].bitcast(FP8X4),
+                    rhs_scale=live[("v_scales", V_LAYOUT[i])][:, cols],
                     start=True,
                     stop=True,
                 )
@@ -400,8 +415,9 @@ def tile_attention_pb_kernel(tc, q_rot, k_rot, v, wo_w, out):
             return None
 
         def w_units_of(tick):
-            first = (tick - W_FIRST_TICK) * W_UNITS_A_TICK
-            return w_units[first : first + W_UNITS_A_TICK] if first >= 0 else []
+            first = int(max(tick - W_FIRST_TICK, 0) * W_UNITS_A_TICK)
+            end = int(max(tick + 1 - W_FIRST_TICK, 0) * W_UNITS_A_TICK)
+            return w_units[first:end]
 
         per_tile = OUT_BANKS * PASSES
         project_from = []
@@ -417,8 +433,10 @@ def tile_attention_pb_kernel(tc, q_rot, k_rot, v, wo_w, out):
         def passes_of(tick):
             found = []
             for k in range(Q_TILES - 1):
+                if (tick - project_from[k]) % 2 == 1:
+                    continue
                 first = (tick - project_from[k]) * PASSES_A_TICK
-                for number in range(max(first, 0), min(first + PASSES_A_TICK, per_tile)):
+                for number in range(max(first, 0), min(first + 2 * PASSES_A_TICK, per_tile)):
                     found.append((TILE_ORDER[k], number // PASSES, number % PASSES))
             for index in range(len(packs)):
                 pack = group_ending_at(index)
@@ -427,60 +445,55 @@ def tile_attention_pb_kernel(tc, q_rot, k_rot, v, wo_w, out):
                         found.extend([(last_tile, nn, pack[1]) for nn in range(OUT_BANKS)])
             return found
 
+        ctx.enter_context(tc.manual_schedule())
         for tick in range(last_tick + 2):
+            pack = group_ending_at(tick - LAG_DIVIDE)
+            if pack is not None:
+                divide(pack[0], pack[1])
             pack = pack_at(tick - LAG_MAX)
             if pack is not None:
                 find_max(pack[0], pack[1], pack[2])
+            pack = group_ending_at(tick - LAG_QUANTISE_E)
+            if pack is not None:
+                quantise_e(pack[0], pack[1])
             pack = pack_at(tick - LAG_EXP)
             if pack is not None:
                 soften(pack[0], pack[1], pack[2])
             for done in passes_of(tick - 1):
                 if done[2] == PASSES - 1:
                     store(done[0], done[1])
-
+            pack = group_ending_at(tick - LAG_QUANTISE_O)
+            if pack is not None:
+                quantise_o(pack[0], pack[1])
+            for unit in w_units_of(tick):
+                if unit[1] == 0 and unit[2] == 0 and 0 < unit[0] < OUT_BANKS - 1:
+                    load_w_chunk(unit[0] + 1)
+                turn_w(unit[0], unit[1], unit[2])
+            pack = pack_at(tick)
+            if pack is not None:
+                score(pack[0], pack[1], pack[2])
             pack = pack_at(tick - LAG_TURN_E)
             if pack is not None and (pack[2] % 2 == 1 or group_ending_at(tick - LAG_TURN_E) is not None):
                 turn_e(pack[0], pack[1], pack[2] - pack[2] % 2, pack[2] % 2 + 1)
             pack = group_ending_at(tick - LAG_TURN_O)
             if pack is not None:
                 turn_o(pack[0], pack[1])
-            for unit in w_units_of(tick):
-                if unit[1] == 0 and unit[2] == 0 and 0 < unit[0] < OUT_BANKS - 1:
-                    load_w_chunk(unit[0] + 1)
-                    if unit[0] + 1 == OUT_BANKS - 1:
-                        load_the_rest()
-                turn_w(unit[0], unit[1], unit[2])
             if tick + 1 < R:
                 turn_q(TILE_ORDER[0], tick + 1)
-            pack = group_ending_at(tick)
+            pack = group_ending_at(tick - LAG_TURN_Q)
             if pack is not None and pack[0] != last_tile:
                 turn_q(TILE_ORDER[TILE_ORDER.index(pack[0]) + 1], pack[1])
-            pack = pack_at(tick)
-            if pack is not None:
-                score(pack[0], pack[1], pack[2])
-
-            pack = group_ending_at(tick - LAG_QUANTISE_E)
-            if pack is not None:
-                quantise_e(pack[0], pack[1])
-            pack = group_ending_at(tick - LAG_DIVIDE)
-            if pack is not None:
-                divide(pack[0], pack[1])
-            pack = group_ending_at(tick - LAG_QUANTISE_O)
-            if pack is not None:
-                quantise_o(pack[0], pack[1])
-            for unit in w_units_of(tick - 1):
-                if unit[2] == ROW_TILES - 1:
-                    quantise_w(unit[0], unit[1])
-
             pack = group_ending_at(tick - LAG_WEIGH)
             if pack is not None:
                 weigh(pack[0], pack[1])
             for due in passes_of(tick):
                 project_pass(due[0], due[1], due[2])
-
-            pack = pack_at(tick - 2)
-            if pack is not None and pack[1] == 0 and pack[2] == 0:
+            for unit in w_units_of(tick - 1):
+                if unit[2] == ROW_TILES - 1:
+                    quantise_w(unit[0], unit[1])
+            pack = group_ending_at(tick - LAG_VALUES - 1)
+            if pack is not None and pack[1] == 0 and V_LAYOUT[pack[0]] == pack[0]:
                 quantise_values(pack[0])
-            pack = pack_at(tick - 1)
-            if pack is not None and pack[1] == 0 and pack[2] == 0:
+            pack = group_ending_at(tick - LAG_VALUES)
+            if pack is not None and pack[1] == 0 and V_LAYOUT[pack[0]] == pack[0]:
                 group_values(pack[0])

@@ -93,8 +93,9 @@ def tile_attention_pb_kernel(tc, q_rot, k_rot, v, wo_w, out):
             pattern=[[-1, P]],
             channel_multiplier=1,
         )
-        mask_bf = keep.tile([P, P], BF16)
-        nc.vector.tensor_copy(out=mask_bf[:], in_=mask_f32[:])
+        mask_bf = keep.tile([P, 2 * P], BF16)
+        nc.vector.memset(mask_bf[:, 0 : 1 * P], 0.0)
+        nc.vector.tensor_copy(out=mask_bf[:, 1 * P :], in_=mask_f32[:])
 
         exp_bias = keep.tile([P, Q_TILES * H], F32)
         row_sum = keep.tile([P, Q_TILES * H], F32)
@@ -198,8 +199,8 @@ def tile_attention_pb_kernel(tc, q_rot, k_rot, v, wo_w, out):
             live[("v_codes", i)] = v_codes
             live[("v_scales", i)] = v_scales
 
-        w_codes = keep.tile([P, PASSES, E], U32, align_bytes=64)
-        w_scales = keep.tile([P, PASSES, E], U8, align_bytes=64)
+        w_codes = keep.tile([P, OUT_BANKS, PASSES, N_OUT], U32, align_bytes=64)
+        w_scales = keep.tile([P, OUT_BANKS, PASSES, N_OUT], U8, align_bytes=64)
 
         def turn_w(nn, half, t):
             if t == 0:
@@ -222,14 +223,12 @@ def tile_attention_pb_kernel(tc, q_rot, k_rot, v, wo_w, out):
             )
 
         def quantise_w(nn, half):
-            for cc in range(2):
-                c = 2 * half + cc
-                cols = slice(nn * N_OUT, (nn + 1) * N_OUT)
-                nc.vector.quantize_mx(
-                    out=w_codes[:, c, cols].bitcast(FP8X4),
-                    scales=w_scales[:, c, cols],
-                    in_=live[("w_grouped", nn, half)][:, cc].rearrange("p n t -> p (n t)"),
-                )
+            passes = slice(2 * half, 2 * half + 2)
+            nc.vector.quantize_mx(
+                out=w_codes[:, nn, passes].rearrange("p c n -> p (c n)").bitcast(FP8X4),
+                scales=w_scales[:, nn, passes].rearrange("p c n -> p (c n)"),
+                in_=live[("w_grouped", nn, half)][:].rearrange("p c n t -> p (c n t)"),
+            )
 
         def score(i, r, pk):
             n = P * (i + 1)
@@ -239,17 +238,18 @@ def tile_attention_pb_kernel(tc, q_rot, k_rot, v, wo_w, out):
             for j in range(hp):
                 g = pk * hp + j
                 queries = live[("qT", i)][:, G * r + g, :]
-                if i > 0:
+                masked = 2 * P if i == TILE_ORDER[0] else P
+                if n > masked:
                     nc.tensor.matmul(
-                        scores[:, j * n : j * n + i * P],
+                        scores[:, j * n : (j + 1) * n - masked],
                         lhsT=queries,
-                        rhs=kT[:, g, 0 : i * P],
+                        rhs=kT[:, g, 0 : n - masked],
                         start=True,
                         stop=True,
                     )
-                diagonal = scores[:, j * n + i * P : (j + 1) * n]
-                nc.tensor.matmul(diagonal, lhsT=queries, rhs=kT[:, g, i * P : n], start=True, stop=False)
-                nc.tensor.matmul(diagonal, lhsT=ident_bf[:], rhs=mask_bf[:], start=False, stop=True)
+                diagonal = scores[:, (j + 1) * n - masked : (j + 1) * n]
+                nc.tensor.matmul(diagonal, lhsT=queries, rhs=kT[:, g, n - masked : n], start=True, stop=False)
+                nc.tensor.matmul(diagonal, lhsT=ident_bf[:], rhs=mask_bf[:, 2 * P - masked :], start=False, stop=True)
 
         def find_max(i, r, pk):
             n = P * (i + 1)
@@ -383,13 +383,12 @@ def tile_attention_pb_kernel(tc, q_rot, k_rot, v, wo_w, out):
                     acc = ps_bank.tile([P, N_OUT], F32, tag="bank")
                 live[("acc", i, nn)] = acc
             rows = slice(c * P, (c + 1) * P)
-            cols = slice(nn * N_OUT, (nn + 1) * N_OUT)
             nc.tensor.matmul_mx(
                 out=live[("acc", i, nn)][:],
                 lhsT=live[("o_codes", i)][:, rows].bitcast(FP8X4),
                 lhsT_scale=live[("o_scales", i)][:, rows],
-                rhs=w_codes[:, c, cols].bitcast(FP8X4),
-                rhs_scale=w_scales[:, c, cols],
+                rhs=w_codes[:, nn, c].bitcast(FP8X4),
+                rhs_scale=w_scales[:, nn, c],
                 start=(c == 0),
                 stop=(c == PASSES - 1),
             )
@@ -428,7 +427,7 @@ def tile_attention_pb_kernel(tc, q_rot, k_rot, v, wo_w, out):
                 if project_from:
                     ready = max(ready, project_from[-1] + per_tile // PASSES_A_TICK)
                 project_from.append(ready)
-        last_tick = max(len(packs) - 1 + LAG_PROJECT, scores_over + 2 * (R - 1), project_from[-1] + per_tile // PASSES_A_TICK)
+        last_tick = max(len(packs) - 1 + LAG_PROJECT, scores_over + 2 + 2 * (R - 1), project_from[-1] + per_tile // PASSES_A_TICK)
 
         def passes_of(tick):
             found = []
@@ -441,7 +440,7 @@ def tile_attention_pb_kernel(tc, q_rot, k_rot, v, wo_w, out):
             for index in range(len(packs)):
                 pack = group_ending_at(index)
                 if pack is not None and pack[0] == last_tile:
-                    if tick == max(index + LAG_PROJECT, scores_over + 2 * pack[1]):
+                    if tick == max(index + LAG_PROJECT, scores_over + 2 + 2 * pack[1]):
                         found.extend([(last_tile, nn, pack[1]) for nn in range(OUT_BANKS)])
             return found
 

import math
from contextlib import ExitStack

import concourse.mybir as mybir
from concourse.masks import make_identity

F32 = mybir.dt.float32
BF16 = mybir.dt.bfloat16
I32 = mybir.dt.int32
U32 = mybir.dt.uint32
U8 = mybir.dt.uint8
FP8X4 = mybir.dt.float8_e4m3fn_x4
ALU = mybir.AluOpType
ACT = mybir.ActivationFunctionType

P = 128
S = 512
H = 16
G = 4
R = H // G
D = 128
E = 2048
Q_TILES = S // P
PASSES = (H * D) // (4 * P)
N_OUT = 512
OUT_BANKS = E // N_OUT
ROW_TILES = N_OUT // P
E_PADDED = 8
V_LAYOUT = (0, 1, 3, 3)
SCORE_BANKS = 3
SCALE = 1.0 / math.sqrt(D)
MASKED = -1.0e30

TILE_ORDER = (3, 0, 1, 2)

LAG_MAX = 1
LAG_EXP = 2
LAG_TURN_E = 3
LAG_QUANTISE_E = 4
LAG_WEIGH = 5
LAG_DIVIDE = 6
LAG_TURN_O = 7
LAG_QUANTISE_O = 8
LAG_TURN_Q = 2
LAG_VALUES = 2
LAG_PROJECT = 9
W_FIRST_TICK = 1
W_UNITS_A_TICK = 1.25
PASSES_A_TICK = 2

FLOPS = 2 * 2 * H * S * S * D + 2 * S * E * H * D


def heads_in_pack(i):
    return S // (P * (i + 1))


def tile_attention_pb_kernel(tc, q_rot, k_rot, v, wo_w, out):
    nc = tc.nc
    with ExitStack() as ctx:
        keep = ctx.enter_context(tc.tile_pool(name="keep", bufs=1))
        stage = ctx.enter_context(tc.tile_pool(name="stage", bufs=2))
        ps_scores = ctx.enter_context(tc.psum_pool(name="ps_scores", bufs=SCORE_BANKS))
        ps_sums = ctx.enter_context(tc.psum_pool(name="ps_sums", bufs=1))
        ps_bank = ctx.enter_context(tc.psum_pool(name="ps_bank", bufs=4))
        live = {}

        e_padded = keep.tile([P, E_PADDED, S], BF16)
        nc.vector.memset(e_padded[:, :, 3 * S // 4 :], 0.0)
        for i in range(2):
            v_slots = keep.tile([P, 4, G * D], BF16, name="v_slots%d" % i)
            nc.vector.memset(v_slots[:].rearrange("p t c -> p (t c)").bitcast(I32), 0)
            live[("v_slots", i)] = v_slots
        v_slots = keep.tile([P, 4, G * D], BF16, name="v_slots%d" % (Q_TILES - 1))
        live[("v_slots", Q_TILES - 1)] = v_slots
        warm_in = keep.tile([P, 1], F32)
        warm_out = keep.tile([P, 1], F32)
        nc.vector.memset(warm_in[:], 0.0)
        nc.scalar.activation(out=warm_out[:], in_=warm_in[:], func=ACT.Exp)

        ident_bf = keep.tile([P, P], BF16)
        make_identity(nc, ident_bf[:])
        ident_f32 = keep.tile([P, P], F32)
        make_identity(nc, ident_f32[:])
        mask_f32 = keep.tile([P, P], F32)
        nc.gpsimd.memset(mask_f32[:], 0.0)
        nc.gpsimd.affine_select(
            out=mask_f32[:],
            in_=mask_f32[:],
            compare_op=ALU.is_ge,
            fill=MASKED,
            base=0,
            pattern=[[-1, P]],
            channel_multiplier=1,
        )
        mask_bf = keep.tile([P, 2 * P], BF16)
        nc.vector.memset(mask_bf[:, 0 : 1 * P], 0.0)
        nc.vector.tensor_copy(out=mask_bf[:, 1 * P :], in_=mask_f32[:])

        exp_bias = keep.tile([P, Q_TILES * H], F32)
        row_sum = keep.tile([P, Q_TILES * H], F32)
        row_inv = keep.tile([P, Q_TILES * H], F32)

        def load_q(i, first, count):
            if first == 0:
                q_rows = keep.tile([P, H * D], BF16, name="q_rows%d" % i)
                live[("q_rows", i)] = q_rows
            nc.sync.dma_start(
                out=live[("q_rows", i)][:, first * D : (first + count) * D],
                in_=q_rot[0, i * P : (i + 1) * P, first : first + count, :].rearrange("s h d -> s (h d)"),
            )

        def load_w_chunk(nn):
            for t in range(ROW_TILES):
                w_rows = stage.tile([P, H * D], BF16, tag="w_rows", bufs=2 * ROW_TILES)
                first = nn * N_OUT + t * P
                nc.sync.dma_start(out=w_rows[:], in_=wo_w[first : first + P, :])
                live[("w_rows", nn, t)] = w_rows

        def load_v(i):
            n = P * (i + 1)
            hp = heads_in_pack(i)
            slots = live[("v_slots", i)]
            for u in range(2):
                keys = v[0, u * (n // 2) : (u + 1) * (n // 2)]
                if hp == 1:
                    nc.sync.dma_start(
                        out=slots[0 : n // 4, 2 * u : 2 * u + 2, :],
                        in_=keys.rearrange("(p e) g d -> p e (g d)", e=2),
                    )
                else:
                    for g in range(G):
                        first = (g % hp) * (P // hp)
                        nc.sync.dma_start(
                            out=slots[first : first + n // 4, 2 * u : 2 * u + 2, g * D : (g + 1) * D],
                            in_=keys[:, g, :].rearrange("(p e) d -> p e d", e=2),
                        )

        load_q(TILE_ORDER[0], 0, G)
        k_rows = keep.tile([P, Q_TILES, G * D], BF16)
        for t in range(Q_TILES):
            nc.sync.dma_start(out=k_rows[:, t, :], in_=k_rot[0, t * P : (t + 1) * P].rearrange("p g d -> p (g d)"))
        for r in range(1, R):
            load_q(TILE_ORDER[0], G * r, G)
        load_w_chunk(0)
        load_v(TILE_ORDER[0])
        load_q(TILE_ORDER[1], 0, H)
        load_w_chunk(1)
        load_v(TILE_ORDER[1])
        for i in TILE_ORDER[2:]:
            load_q(i, 0, H)
            if V_LAYOUT[i] == i:
                load_v(i)

        def turn_q(i, r):
            if r == 0:
                qT = keep.tile([P, H, P], BF16, name="qT%d" % i)
                live[("qT", i)] = qT
            turned = ps_bank.tile([P, G, P], BF16, tag="bank")
            for g in range(G):
                h = G * r + g
                nc.tensor.transpose(turned[:, g, :], live[("q_rows", i)][:, h * D : (h + 1) * D], ident_bf[:])
            nc.scalar.copy(out=live[("qT", i)][:, G * r : G * (r + 1), :], in_=turned[:])

        turn_q(TILE_ORDER[0], 0)

        kT = keep.tile([P, G, S], BF16)
        k_turned = []
        for g in range(G):
            bank = ps_bank.tile([P, Q_TILES, P], BF16, tag="bank")
            k_turned.append(bank)
        for t in range(Q_TILES):
            for g in range(G):
                nc.tensor.transpose(k_turned[g][:, t, :], k_rows[:, t, g * D : (g + 1) * D], ident_bf[:])
        for g in range(G):
            copy = nc.vector.tensor_copy if g % 2 == 0 else nc.scalar.copy
            copy(out=kT[:, g, :], in_=k_turned[g][:].rearrange("p t s -> p (t s)"))

        def group_values(i):
            v_grouped = stage.tile([P, G * D, 4], BF16, tag="v_grouped", align_bytes=64)
            nc.gpsimd.tensor_scalar(
                out=v_grouped[:],
                in0=live[("v_slots", i)][:].rearrange("p t c -> p c t"),
                scalar1=1.0,
                scalar2=0.0,
                op0=ALU.mult,
                op1=ALU.add,
            )
            live[("v_grouped", i)] = v_grouped

        def quantise_values(i):
            v_codes = keep.tile([P, G * D], U32, name="v_codes%d" % i, align_bytes=64)
            v_scales = keep.tile([P, G * D], U8, name="v_scales%d" % i, align_bytes=64)
            nc.vector.quantize_mx(
                out=v_codes[:].bitcast(FP8X4),
                scales=v_scales[:],
                in_=live[("v_grouped", i)][:].rearrange("p c t -> p (c t)"),
            )
            live[("v_codes", i)] = v_codes
            live[("v_scales", i)] = v_scales

        w_codes = keep.tile([P, OUT_BANKS, PASSES, N_OUT], U32, align_bytes=64)
        w_scales = keep.tile([P, OUT_BANKS, PASSES, N_OUT], U8, align_bytes=64)

        def turn_w(nn, half, t):
            if t == 0:
                w_grouped = stage.tile([P, 2, N_OUT, 4], BF16, tag="w_grouped", align_bytes=64)
                live[("w_grouped", nn, half)] = w_grouped
            words = live[("w_rows", nn, t)][:].bitcast(F32)
            turned = ps_bank.tile([P, 2, 2, P], F32, tag="bank")
            for cc in range(2):
                c = 2 * half + cc
                for u in range(2):
                    nc.tensor.transpose(
                        turned[:, cc, u, :], words[:, 256 * c + u : 256 * (c + 1) : 2], ident_f32[:]
                    )
            grouped_words = live[("w_grouped", nn, half)][:].rearrange("p c n t -> p (c n t)").bitcast(F32)
            grouped_words = grouped_words.rearrange("p (c n u) -> p c n u", c=2, u=2)
            copy = nc.vector.tensor_copy if t == ROW_TILES - 1 else nc.scalar.copy
            copy(
                out=grouped_words[:, :, t * P : (t + 1) * P, :],
                in_=turned[:].rearrange("p c u n -> p c n u"),
            )

        def quantise_w(nn, half):
            passes = slice(2 * half, 2 * half + 2)
            nc.vector.quantize_mx(
                out=w_codes[:, nn, passes].rearrange("p c n -> p (c n)").bitcast(FP8X4),
                scales=w_scales[:, nn, passes].rearrange("p c n -> p (c n)"),
                in_=live[("w_grouped", nn, half)][:].rearrange("p c n t -> p (c n t)"),
            )

        def score(i, r, pk):
            n = P * (i + 1)
            hp = heads_in_pack(i)
            scores = ps_scores.tile([P, S], F32, tag="scores")
            live[("scores", i, r, pk)] = scores
            for j in range(hp):
                g = pk * hp + j
                queries = live[("qT", i)][:, G * r + g, :]
                masked = 2 * P if i == TILE_ORDER[0] else P
                if n > masked:
                    nc.tensor.matmul(
                        scores[:, j * n : (j + 1) * n - masked],
                        lhsT=queries,
                        rhs=kT[:, g, 0 : n - masked],
                        start=True,
                        stop=True,
                    )
                diagonal = scores[:, (j + 1) * n - masked : (j + 1) * n]
                nc.tensor.matmul(diagonal, lhsT=queries, rhs=kT[:, g, n - masked : n], start=True, stop=False)
                nc.tensor.matmul(diagonal, lhsT=ident_bf[:], rhs=mask_bf[:, 2 * P - masked :], start=False, stop=True)

        def find_max(i, r, pk):
            n = P * (i + 1)
            hp = heads_in_pack(i)
            col = i * H + G * r + pk * hp
            scaled = stage.tile([P, S], F32, tag="scaled", bufs=4)
            live[("scaled", i, r, pk)] = scaled
            for j in range(hp):
                nc.vector.tensor_scalar(
                    out=scaled[:, j * n : (j + 1) * n],
                    in0=live[("scores", i, r, pk)][:, j * n : (j + 1) * n],
                    scalar1=-SCALE,
                    scalar2=None,
                    op0=ALU.mult,
                    op1=ALU.min,
                    accum_out=exp_bias[:, col + j : col + j + 1],
                )

        def soften(i, r, pk):
            n = P * (i + 1)
            hp = heads_in_pack(i)
            col = i * H + G * r + pk * hp
            scaled = live[("scaled", i, r, pk)]
            if n * hp < S:
                e_tile = e_padded[:, (G * r + pk) % E_PADDED]
            else:
                e_fresh = stage.tile([P, S], BF16, tag="e_tile", bufs=6)
                e_tile = e_fresh[:]
            live[("e", i, r, pk)] = e_tile
            e_view = e_tile.rearrange("p (u j k) -> p u j k", u=2, j=hp)
            for j in range(hp):
                exponents = scaled[:, j * n : (j + 1) * n]
                nc.scalar.activation(
                    out=e_tile[:, 0:n] if hp == 1 else e_view[:, :, j],
                    in_=exponents if hp == 1 else exponents.rearrange("p (u k) -> p u k", u=2),
                    func=ACT.Exp,
                    bias=exp_bias[:, col + j : col + j + 1],
                    scale=-1.0,
                    accum_out=row_sum[:, col + j : col + j + 1],
                )

        def turn_e(i, r, first, count):
            if first == 0:
                e_grouped = stage.tile([P, G * 4 * P], BF16, tag="e_grouped", align_bytes=64)
                live[("e_grouped", i, r)] = e_grouped
            e_words = live[("e_grouped", i, r)][:].bitcast(F32).rearrange("p (s q u) -> p s q u", s=G, u=2)
            turned = ps_bank.tile([P, 2, 2, P], F32, tag="bank")
            for s in range(count):
                words = live[("e", i, r, first + s)].bitcast(F32)
                for u in range(2):
                    nc.tensor.transpose(turned[:, s, u, :], words[:, u * P : (u + 1) * P], ident_f32[:])
            nc.scalar.copy(
                out=e_words[:, first : first + count],
                in_=turned[:, 0:count].rearrange("p s u q -> p s q u"),
            )

        def quantise_e(i, r):
            packs_here = G // heads_in_pack(i)
            col = i * H + G * r
            nc.vector.reciprocal(out=row_inv[:, col : col + G], in_=row_sum[:, col : col + G])
            e_codes = stage.tile([P, G * P], U32, tag="e_codes", align_bytes=64)
            e_scales = stage.tile([P, G * P], U8, tag="e_scales", align_bytes=64)
            nc.vector.quantize_mx(
                out=e_codes[:, 0 : packs_here * P].bitcast(FP8X4),
                scales=e_scales[:, 0 : packs_here * P],
                in_=live[("e_grouped", i, r)][:, 0 : packs_here * 4 * P],
            )
            live[("e_codes", i, r)] = e_codes
            live[("e_scales", i, r)] = e_scales

        def weigh(i, r):
            hp = heads_in_pack(i)
            sums = ps_sums.tile([P, G * D], F32, tag="sums")
            live[("sums", i, r)] = sums
            for pk in range(G // hp):
                rows = slice(pk * P, (pk + 1) * P)
                cols = slice(pk * hp * D, (pk + 1) * hp * D)
                nc.tensor.matmul_mx(
                    out=sums[:, cols],
                    lhsT=live[("e_codes", i, r)][:, rows].bitcast(FP8X4),
                    lhsT_scale=live[("e_scales", i, r)][:, rows],
                    rhs=live[("v_codes", V_LAYOUT[i])][:, cols].bitcast(FP8X4),
                    rhs_scale=live[("v_scales", V_LAYOUT[i])][:, cols],
                    start=True,
                    stop=True,
                )

        def divide(i, r):
            col = i * H + G * r
            if r == 0:
                o_sorted = stage.tile([P, PASSES, 2, 2 * P], BF16, tag="o_sorted")
                live[("o_sorted", i)] = o_sorted
            sums_view = live[("sums", i, r)][:].rearrange("q (g p u e) -> q u g p e", g=G, u=2, e=2)
            inv_view = row_inv[:, col : col + G].unsqueeze(2).unsqueeze(3).to_broadcast([P, G, D // 4, 2])
            for u in range(2):
                nc.vector.tensor_tensor(
                    out=live[("o_sorted", i)][:, r, u, :].rearrange("q (g p e) -> q g p e", g=G, e=2),
                    in0=sums_view[:, u],
                    in1=inv_view,
                    op=ALU.mult,
                )

        def turn_o(i, r):
            if r == 0:
                o_grouped = stage.tile([P, PASSES * 4 * P], BF16, tag="o_grouped", align_bytes=64)
                live[("o_grouped", i)] = o_grouped
            turned = ps_bank.tile([P, 2, P], F32, tag="bank")
            words = live[("o_sorted", i)][:, r].rearrange("q u k -> q (u k)").bitcast(F32)
            for u in range(2):
                nc.tensor.transpose(turned[:, u, :], words[:, u * P : (u + 1) * P], ident_f32[:])
            o_words = live[("o_grouped", i)][:].bitcast(F32).rearrange("p (c q u) -> p c q u", c=PASSES, u=2)
            nc.scalar.copy(out=o_words[:, r], in_=turned[:].rearrange("p u q -> p q u"))

        def quantise_o(i, r):
            if r == 0:
                o_codes = stage.tile([P, PASSES * P], U32, tag="o_codes", align_bytes=64, bufs=3)
                o_scales = stage.tile([P, PASSES * P], U8, tag="o_scales", align_bytes=64, bufs=3)
                live[("o_codes", i)] = o_codes
                live[("o_scales", i)] = o_scales
            nc.vector.quantize_mx(
                out=live[("o_codes", i)][:, r * P : (r + 1) * P].bitcast(FP8X4),
                scales=live[("o_scales", i)][:, r * P : (r + 1) * P],
                in_=live[("o_grouped", i)][:, r * 4 * P : (r + 1) * 4 * P],
            )

        def project_pass(i, nn, c):
            if c == 0:
                if i == TILE_ORDER[-1] and nn < SCORE_BANKS:
                    acc = ps_scores.tile([P, N_OUT], F32, tag="scores")
                else:
                    acc = ps_bank.tile([P, N_OUT], F32, tag="bank")
                live[("acc", i, nn)] = acc
            rows = slice(c * P, (c + 1) * P)
            nc.tensor.matmul_mx(
                out=live[("acc", i, nn)][:],
                lhsT=live[("o_codes", i)][:, rows].bitcast(FP8X4),
                lhsT_scale=live[("o_scales", i)][:, rows],
                rhs=w_codes[:, nn, c].bitcast(FP8X4),
                rhs_scale=w_scales[:, nn, c],
                start=(c == 0),
                stop=(c == PASSES - 1),
            )

        def store(i, nn):
            result = stage.tile([P, N_OUT], F32, tag="result", bufs=4)
            copy = nc.vector.tensor_copy if i == TILE_ORDER[-1] and nn % 2 == 1 else nc.scalar.copy
            copy(out=result[:], in_=live[("acc", i, nn)][:])
            nc.sync.dma_start(out=out[0, i * P : (i + 1) * P, nn * N_OUT : (nn + 1) * N_OUT], in_=result[:])

        packs = [(i, r, pk) for i in TILE_ORDER for r in range(R) for pk in range(G // heads_in_pack(i))]
        w_units = [(nn, half, t) for nn in range(OUT_BANKS) for half in range(2) for t in range(ROW_TILES)]
        last_tile = TILE_ORDER[-1]
        scores_over = len(packs) + LAG_MAX

        def pack_at(index):
            return packs[index] if 0 <= index < len(packs) else None

        def group_ending_at(index):
            pack = pack_at(index)
            if pack is not None and pack[2] == G // heads_in_pack(pack[0]) - 1:
                return pack
            return None

        def w_units_of(tick):
            first = int(max(tick - W_FIRST_TICK, 0) * W_UNITS_A_TICK)
            end = int(max(tick + 1 - W_FIRST_TICK, 0) * W_UNITS_A_TICK)
            return w_units[first:end]

        per_tile = OUT_BANKS * PASSES
        project_from = []
        for index in range(len(packs)):
            pack = group_ending_at(index)
            if pack is not None and pack[1] == R - 1 and pack[0] != last_tile:
                ready = index + LAG_PROJECT
                if project_from:
                    ready = max(ready, project_from[-1] + per_tile // PASSES_A_TICK)
                project_from.append(ready)
        last_tick = max(len(packs) - 1 + LAG_PROJECT, scores_over + 2 + 2 * (R - 1), project_from[-1] + per_tile // PASSES_A_TICK)

        def passes_of(tick):
            found = []
            for k in range(Q_TILES - 1):
                if (tick - project_from[k]) % 2 == 1:
                    continue
                first = (tick - project_from[k]) * PASSES_A_TICK
                for number in range(max(first, 0), min(first + 2 * PASSES_A_TICK, per_tile)):
                    found.append((TILE_ORDER[k], number // PASSES, number % PASSES))
            for index in range(len(packs)):
                pack = group_ending_at(index)
                if pack is not None and pack[0] == last_tile:
                    if tick == max(index + LAG_PROJECT, scores_over + 2 + 2 * pack[1]):
                        found.extend([(last_tile, nn, pack[1]) for nn in range(OUT_BANKS)])
            return found

        ctx.enter_context(tc.manual_schedule())
        for tick in range(last_tick + 2):
            pack = group_ending_at(tick - LAG_DIVIDE)
            if pack is not None:
                divide(pack[0], pack[1])
            pack = pack_at(tick - LAG_MAX)
            if pack is not None:
                find_max(pack[0], pack[1], pack[2])
            pack = group_ending_at(tick - LAG_QUANTISE_E)
            if pack is not None:
                quantise_e(pack[0], pack[1])
            pack = pack_at(tick - LAG_EXP)
            if pack is not None:
                soften(pack[0], pack[1], pack[2])
            for done in passes_of(tick - 1):
                if done[2] == PASSES - 1:
                    store(done[0], done[1])
            pack = group_ending_at(tick - LAG_QUANTISE_O)
            if pack is not None:
                quantise_o(pack[0], pack[1])
            for unit in w_units_of(tick):
                if unit[1] == 0 and unit[2] == 0 and 0 < unit[0] < OUT_BANKS - 1:
                    load_w_chunk(unit[0] + 1)
                turn_w(unit[0], unit[1], unit[2])
            pack = pack_at(tick)
            if pack is not None:
                score(pack[0], pack[1], pack[2])
            pack = pack_at(tick - LAG_TURN_E)
            if pack is not None and (pack[2] % 2 == 1 or group_ending_at(tick - LAG_TURN_E) is not None):
                turn_e(pack[0], pack[1], pack[2] - pack[2] % 2, pack[2] % 2 + 1)
            pack = group_ending_at(tick - LAG_TURN_O)
            if pack is not None:
                turn_o(pack[0], pack[1])
            if tick + 1 < R:
                turn_q(TILE_ORDER[0], tick + 1)
            pack = group_ending_at(tick - LAG_TURN_Q)
            if pack is not None and pack[0] != last_tile:
                turn_q(TILE_ORDER[TILE_ORDER.index(pack[0]) + 1], pack[1])
            pack = group_ending_at(tick - LAG_WEIGH)
            if pack is not None:
                weigh(pack[0], pack[1])
            for due in passes_of(tick):
                project_pass(due[0], due[1], due[2])
            for unit in w_units_of(tick - 1):
                if unit[2] == ROW_TILES - 1:
                    quantise_w(unit[0], unit[1])
            pack = group_ending_at(tick - LAG_VALUES - 1)
            if pack is not None and pack[1] == 0 and V_LAYOUT[pack[0]] == pack[0]:
                quantise_values(pack[0])
            pack = group_ending_at(tick - LAG_VALUES)
            if pack is not None and pack[1] == 0 and V_LAYOUT[pack[0]] == pack[0]:
                group_values(pack[0])
